import numpy as np
import ml_dtypes


def mxq(x, axis, fmt="e4m3"):
    dtype, down = {"e4m3": (ml_dtypes.float8_e4m3fn, 7), "e5m2": (ml_dtypes.float8_e5m2, 14)}[fmt]
    v = np.moveaxis(np.asarray(x, np.float32).astype(ml_dtypes.bfloat16).astype(np.float64), axis, -1)
    blocks = v.reshape(v.shape[:-1] + (-1, 32))
    amax = np.abs(blocks).max(-1, keepdims=True)
    byte = np.maximum(np.where(amax > 0, np.frexp(amax)[1] - 1 + 127, 0) - down, 1)
    scale = np.exp2(byte - 127.0)
    codes = (blocks / scale).astype(np.float32).astype(dtype).astype(np.float64)
    return np.moveaxis((codes * scale).reshape(v.shape), -1, axis)


WIDE = False


def mx_kscale(k):
    if not WIDE:
        return np.ones(k)
    levels = np.array([10, -10, 5, -5, 0])
    a = np.random.permutation(np.resize(levels, k // 512 * 4)).reshape(k // 512, 4)
    idx = np.arange(k)
    return np.exp2(a[idx // 512, idx % 128 // 32])


BF16 = ml_dtypes.bfloat16


def bf(x):
    return np.asarray(x, np.float32).astype(BF16)


def f64(x):
    return np.asarray(x).astype(np.float64)


N, N_CH, X, H = 4096, 4, 512, 256
K = N_CH * H
G = 3 * H


def sigmoid(v):
    return 1.0 / (1.0 + np.exp(-v))


def setup_inputs():
    s, t = mx_kscale(X), mx_kscale(K)
    return {
        "x": bf(np.random.standard_normal((N, X)) * s),
        "x_mask": bf(np.random.random(N) < 0.75),
        "neighbour_h": bf(np.random.standard_normal((N, N_CH, H)) * t.reshape(N_CH, H)),
        "c_aggr": bf(np.random.standard_normal((N, H)) * 0.57 * np.sqrt(N_CH)),
        "W_iou_in": bf(np.random.standard_normal((X, G)) / np.sqrt(X) / s[:, None]),
        "b_iou_in": bf(np.random.standard_normal(G) * 0.3),
        "W_aggr_iou": bf(np.random.standard_normal((K, G)) / np.sqrt(K) / t[:, None]),
        "b_aggr_iou": bf(np.random.standard_normal(G) * 0.3),
    }


def reference(x, x_mask, neighbour_h, c_aggr, W_iou_in, b_iou_in, W_aggr_iou, b_aggr_iou):
    h_flat = f64(neighbour_h).reshape(N, K)
    iou_aggr = (mxq(h_flat, 1, "e4m3") @ mxq(f64(W_aggr_iou), 0, "e4m3")) + f64(b_aggr_iou)
    iou = ((mxq(f64(x), 1, "e4m3") @ mxq(f64(W_iou_in), 0, "e4m3")) + f64(b_iou_in)) * f64(x_mask)[:, None] + iou_aggr
    i, o, u = np.split(iou, 3, axis=1)
    i, o, u = sigmoid(i), sigmoid(o), np.tanh(u)
    c = i * u + f64(c_aggr)
    h = o * np.tanh(c)
    return h, c

@@ -1,0 +1,278 @@
+from contextlib import ExitStack
+
+import concourse.mybir as mybir
+from concourse.masks import make_identity
+
+BF16 = mybir.dt.bfloat16
+F32 = mybir.dt.float32
+U32 = mybir.dt.uint32
+U8 = mybir.dt.uint8
+FP8X4 = mybir.dt.float8_e4m3fn_x4
+ACT = mybir.ActivationFunctionType
+ALU = mybir.AluOpType
+
+P = 128
+PACK = 4
+K_PASS = P * PACK
+NODES, X_DIM, CHILDREN, H_DIM = 4096, 512, 4, 256
+HF_DIM = CHILDREN * H_DIM
+GATES = 3 * H_DIM
+PASSES = (X_DIM + HF_DIM) // K_PASS
+GATE_TILES = GATES // P
+H_TILES = H_DIM // P
+NODE_TILES = NODES // P
+CHUNK = 512
+CHUNK_TILES = CHUNK // P
+CHUNKS = NODES // CHUNK
+WORDS = P
+BANK_TILES = 2
+TP_BANKS = PASSES * CHUNK_TILES // BANK_TILES
+GATE_ORDER = (0, 1, 4, 5, 2, 3)
+
+FLOPS = 2 * NODES * (X_DIM + HF_DIM) * GATES
+
+
+def tile_treelstmcell_pb_t_kernel(
+    tc, x, x_mask, neighbour_h, c_aggr, W_iou_in, b_iou_in, W_aggr_iou, b_aggr_iou, out_0, out_1
+):
+    nc = tc.nc
+
+    x_rows = x.rearrange("(p t) k -> p (t k)", t=NODE_TILES)
+    hf_rows = neighbour_h.rearrange("(p t) c f -> p (t c f)", t=NODE_TILES)
+    c_aggr_rows = c_aggr.rearrange("(p t) f -> p t f", t=NODE_TILES)
+    h_rows = out_0.rearrange("(p t) f -> p t f", t=NODE_TILES)
+    c_rows = out_1.rearrange("(p t) f -> p t f", t=NODE_TILES)
+
+    with ExitStack() as ctx:
+        const = ctx.enter_context(tc.tile_pool(name="const", bufs=1))
+        wstage = ctx.enter_context(tc.tile_pool(name="wstage", bufs=3))
+        loads = ctx.enter_context(tc.tile_pool(name="loads", bufs=3))
+        acts = ctx.enter_context(tc.tile_pool(name="acts", bufs=2))
+        work = ctx.enter_context(tc.tile_pool(name="work", bufs=2))
+        psum_tp = ctx.enter_context(tc.psum_pool(name="psum_tp", bufs=3))
+        psum_z = ctx.enter_context(tc.psum_pool(name="psum_z", bufs=3))
+        psum_bt = ctx.enter_context(tc.psum_pool(name="psum_bt", bufs=2))
+
+        ctx.enter_context(tc.manual_schedule())
+
+        x_sb, hf_sb, c_aggr_sb, diag = {}, {}, {}, {}
+        w_raw, w_grouped = {}, {}
+        a_grouped, a_codes, a_scales = {}, {}, {}
+        gates, i_times_u, c_new, tanh_c = {}, {}, {}, {}
+
+        ident = const.tile([P, P], F32)
+        make_identity(nc, ident[:])
+        ident_bf = const.tile([P, P], BF16)
+        make_identity(nc, ident_bf[:])
+
+        mask_col = const.tile([P, NODE_TILES], BF16)
+        nc.sync.dma_start(out=mask_col[:], in_=x_mask.rearrange("(p t) -> p t", t=NODE_TILES))
+        mask_all = const.tile([P, NODES], BF16)
+        mask_row = const.tile([P, NODE_TILES, P], BF16)
+
+        def load(c):
+            tiles = slice(c * CHUNK_TILES, (c + 1) * CHUNK_TILES)
+            x_sb[c] = loads.tile([P, CHUNK_TILES * X_DIM], BF16, name="x_sb")
+            nc.sync.dma_start(out=x_sb[c][:], in_=x_rows[:, c * CHUNK_TILES * X_DIM : (c + 1) * CHUNK_TILES * X_DIM])
+            hf_sb[c] = loads.tile([P, CHUNK_TILES * HF_DIM], BF16, name="hf_sb")
+            nc.sync.dma_start(
+                out=hf_sb[c][:], in_=hf_rows[:, c * CHUNK_TILES * HF_DIM : (c + 1) * CHUNK_TILES * HF_DIM]
+            )
+            c_aggr_sb[c] = loads.tile([P, CHUNK_TILES, H_DIM], BF16, name="c_aggr_sb", bufs=4)
+            nc.sync.dma_start(out=c_aggr_sb[c][:], in_=c_aggr_rows[:, tiles, :])
+            diag[c] = loads.tile([P, CHUNK_TILES, P], F32, name="diag")
+            nc.gpsimd.tensor_tensor(
+                out=diag[c][:],
+                in0=ident[:].unsqueeze(1).to_broadcast([P, CHUNK_TILES, P]),
+                in1=mask_col[:, tiles].unsqueeze(2).to_broadcast([P, CHUNK_TILES, P]),
+                op=ALU.mult,
+            )
+
+        def order_mask(c):
+            tiles = slice(c * CHUNK_TILES, (c + 1) * CHUNK_TILES)
+            nc.gpsimd.tensor_scalar(
+                out=mask_row[:, tiles, :],
+                in0=mask_all[:].rearrange("q (p t) -> q t p", t=NODE_TILES)[:, tiles, :],
+                scalar1=1.0,
+                scalar2=0.0,
+                op0=ALU.mult,
+                op1=ALU.add,
+            )
+
+        def transpose_in(c, banks):
+            if c not in a_grouped:
+                a_grouped[c] = acts.tile([P, PASSES * CHUNK * PACK], BF16, name="a_grouped", align_bytes=64)
+            x_words = x_sb[c][:].bitcast(F32)
+            hf_words = hf_sb[c][:].bitcast(F32)
+            grouped_words = a_grouped[c][:].bitcast(F32)
+            for b in banks:
+                g, half = divmod(b, CHUNK_TILES // BANK_TILES)
+                kT = psum_tp.tile([P, 2, BANK_TILES * P], F32, name="kT")
+                for jj in range(BANK_TILES):
+                    j = half * BANK_TILES + jj
+                    for u in range(2):
+                        if g == 0:
+                            first = j * (X_DIM // 2) + u * WORDS
+                            words, perm = x_words[:, first : first + WORDS], diag[c][:, j, :]
+                        else:
+                            first = j * (HF_DIM // 2) + (g - 1) * (K_PASS // 2) + u * WORDS
+                            words, perm = hf_words[:, first : first + WORDS], ident[:]
+                        nc.tensor.transpose(kT[:, u, jj * P : (jj + 1) * P], words, perm)
+                first = (g * CHUNK + half * BANK_TILES * P) * 2
+                nc.scalar.copy(
+                    out=grouped_words[:, first : first + BANK_TILES * P * 2].rearrange("p (n u) -> p n u", u=2),
+                    in_=kT[:].rearrange("p u n -> p n u"),
+                )
+
+        def quantise(c, first_pass, passes):
+            if c not in a_codes:
+                a_codes[c] = acts.tile([P, PASSES * CHUNK], U32, name="a_codes", align_bytes=64)
+                a_scales[c] = acts.tile([P, PASSES * CHUNK], U8, name="a_scales", align_bytes=64)
+            cols = slice(first_pass * CHUNK, (first_pass + passes) * CHUNK)
+            nc.vector.quantize_mx(
+                out=a_codes[c][:, cols].bitcast(FP8X4),
+                scales=a_scales[c][:, cols],
+                in_=a_grouped[c][:, first_pass * CHUNK * PACK : (first_pass + passes) * CHUNK * PACK],
+            )
+
+        def gate_tiles(c, some):
+            if c not in gates:
+                gates[c] = work.tile([P, GATE_TILES, CHUNK], F32, name="gates")
+            for m in some:
+                sums = psum_z.tile([P, CHUNK], F32, name="sums")
+                for g in range(PASSES):
+                    w_cols = slice(g * GATES + m * P, g * GATES + (m + 1) * P)
+                    a_cols = slice(g * CHUNK, (g + 1) * CHUNK)
+                    nc.tensor.matmul_mx(
+                        out=sums[:],
+                        lhsT=w_codes[:, w_cols].bitcast(FP8X4),
+                        lhsT_scale=w_scales[:, w_cols],
+                        rhs=a_codes[c][:, a_cols].bitcast(FP8X4),
+                        rhs_scale=a_scales[c][:, a_cols],
+                        start=(g == 0),
+                        stop=(g == PASSES - 1),
+                    )
+                masked = work.tile([P, CHUNK], F32, name="masked", bufs=4)
+                nc.vector.scalar_tensor_tensor(
+                    out=masked[:],
+                    in0=mask_row[:, c * CHUNK_TILES : (c + 1) * CHUNK_TILES, :].rearrange("q t p -> q (t p)"),
+                    scalar=bias_col[:, m : m + 1],
+                    in1=sums[:],
+                    op0=ALU.mult,
+                    op1=ALU.add,
+                )
+                nc.scalar.activation(
+                    out=gates[c][:, m, :],
+                    in_=masked[:],
+                    func=(ACT.Tanh if m >= 2 * H_TILES else ACT.Sigmoid),
+                    bias=bias_col[:, GATE_TILES + m : GATE_TILES + m + 1],
+                    scale=1.0,
+                )
+
+        def multiply_i_u(c):
+            i_times_u[c] = work.tile([P, H_TILES, CHUNK], F32, name="i_times_u")
+            nc.gpsimd.tensor_tensor(
+                out=i_times_u[c][:],
+                in0=gates[c][:, 0:H_TILES, :],
+                in1=gates[c][:, 2 * H_TILES : 3 * H_TILES, :],
+                op=ALU.mult,
+            )
+
+        def transpose_back(source, first_tile, half):
+            back = psum_bt.tile([P, BANK_TILES, H_DIM], F32, name="back")
+            for jj in range(BANK_TILES):
+                j = half * BANK_TILES + jj
+                for f in range(H_TILES):
+                    nc.tensor.transpose(
+                        back[:, jj, f * P : (f + 1) * P], source[:, first_tile + f, j * P : (j + 1) * P], ident[:]
+                    )
+            return back
+
+        def cell_state(c):
+            c_new[c] = work.tile([P, CHUNK_TILES, H_DIM], F32, name="c_new", bufs=3)
+            tanh_c[c] = work.tile([P, CHUNK_TILES, H_DIM], F32, name="tanh_c")
+            for half in range(CHUNK_TILES // BANK_TILES):
+                tiles = slice(half * BANK_TILES, (half + 1) * BANK_TILES)
+                back = transpose_back(i_times_u[c], 0, half)
+                nc.vector.tensor_tensor(out=c_new[c][:, tiles, :], in0=back[:], in1=c_aggr_sb[c][:, tiles, :], op=ALU.add)
+            nc.scalar.activation(out=tanh_c[c][:], in_=c_new[c][:], func=ACT.Tanh)
+            nc.sync.dma_start(out=c_rows[:, c * CHUNK_TILES : (c + 1) * CHUNK_TILES, :], in_=c_new[c][:])
+
+        def hidden_state(c):
+            h_new = work.tile([P, CHUNK_TILES, H_DIM], F32, name="h_new", bufs=3)
+            for half in range(CHUNK_TILES // BANK_TILES):
+                tiles = slice(half * BANK_TILES, (half + 1) * BANK_TILES)
+                back = transpose_back(gates[c], H_TILES, half)
+                nc.vector.tensor_tensor(out=h_new[:, tiles, :], in0=back[:], in1=tanh_c[c][:, tiles, :], op=ALU.mult)
+            nc.sync.dma_start(out=h_rows[:, c * CHUNK_TILES : (c + 1) * CHUNK_TILES, :], in_=h_new[:])
+
+        w_codes = const.tile([P, PASSES * GATES], U32, align_bytes=64)
+        w_scales = const.tile([P, PASSES * GATES], U8, align_bytes=64)
+
+        def load_weights(g):
+            rows = W_iou_in if g == 0 else W_aggr_iou[(g - 1) * K_PASS : g * K_PASS, :]
+            w_raw[g] = wstage.tile([P, PACK, GATES], BF16, name="w_raw")
+            nc.sync.dma_start(
+                out=w_raw[g][:].rearrange("q (u e) c -> q u (e c)", u=2),
+                in_=rows.rearrange("(u q e) c -> q u (e c)", u=2, e=2),
+            )
+
+        def group_weights(g):
+            w_grouped[g] = wstage.tile([P, GATES, PACK], BF16, name="w_grouped", align_bytes=64)
+            nc.vector.tensor_copy(out=w_grouped[g][:], in_=w_raw[g][:].rearrange("q t c -> q c t"))
+
+        def quantise_weights(g):
+            for first, cols in ((0, 512), (512, 256)):
+                nc.vector.quantize_mx(
+                    out=w_codes[:, g * GATES + first : g * GATES + first + cols].bitcast(FP8X4),
+                    scales=w_scales[:, g * GATES + first : g * GATES + first + cols],
+                    in_=w_grouped[g][:].rearrange("q c t -> q (c t)")[:, first * PACK : (first + cols) * PACK],
+                )
+
+        bias_rows = const.tile([P, P], BF16)
+        nc.vector.memset(bias_rows[:], 0.0)
+        for g in range(PASSES):
+            load_weights(g)
+        load(0)
+        nc.sync.dma_start(out=bias_rows[0:GATE_TILES, :], in_=b_iou_in.rearrange("(m g) -> m g", g=P))
+        nc.sync.dma_start(out=bias_rows[GATE_TILES : 2 * GATE_TILES, :], in_=b_aggr_iou.rearrange("(m g) -> m g", g=P))
+        nc.sync.dma_start(out=mask_all[:], in_=x_mask.partition_broadcast(P))
+        load(1)
+
+        group_weights(0)
+        for g in range(1, PASSES):
+            group_weights(g)
+            quantise_weights(g - 1)
+        quantise_weights(PASSES - 1)
+
+        transpose_in(0, range(TP_BANKS))
+        quantise(0, 0, 1)
+        quantise(0, 1, 2)
+        order_mask(0)
+
+        bias_ps = psum_bt.tile([P, P], BF16, name="bias_ps", tag="back")
+        nc.tensor.transpose(bias_ps[:], bias_rows[:], ident_bf[:])
+        bias_col = const.tile([P, 2 * GATE_TILES], F32)
+        nc.vector.tensor_copy(out=bias_col[:], in_=bias_ps[:, 0 : 2 * GATE_TILES])
+
+        for c in range(CHUNKS + 2):
+            if c + 2 < CHUNKS:
+                load(c + 2)
+            if c + 1 < CHUNKS:
+                order_mask(c + 1)
+                transpose_in(c + 1, range(0, TP_BANKS // 2))
+            if 0 <= c - 2:
+                hidden_state(c - 2)
+            if c + 1 < CHUNKS:
+                quantise(c + 1, 0, 1)
+            if c < CHUNKS:
+                gate_tiles(c, GATE_ORDER[0 : GATE_TILES // 2])
+            if c + 1 < CHUNKS:
+                transpose_in(c + 1, range(TP_BANKS // 2, TP_BANKS))
+            if 0 <= c - 1 < CHUNKS:
+                cell_state(c - 1)
+            if c < CHUNKS:
+                gate_tiles(c, GATE_ORDER[GATE_TILES // 2 :])
+                multiply_i_u(c)
+            if c + 1 < CHUNKS:
+                quantise(c + 1, 1, 2)

@@ -55,7 +55,7 @@ def tile_treelstmcell_pb_t_kernel(
 
         ctx.enter_context(tc.manual_schedule())
 
-        x_sb, hf_sb, c_aggr_sb, diag = {}, {}, {}, {}
+        x_sb, hf_sb, c_aggr_sb = {}, {}, {}
         w_raw, w_grouped = {}, {}
         a_grouped, a_codes, a_scales = {}, {}, {}
         gates, i_times_u, c_new, tanh_c = {}, {}, {}, {}
@@ -70,19 +70,24 @@ def tile_treelstmcell_pb_t_kernel(
         mask_all = const.tile([P, NODES], BF16)
         mask_row = const.tile([P, NODE_TILES, P], BF16)
 
+        diag = const.tile([P, NODE_TILES, P], F32)
+
         def load(c):
-            tiles = slice(c * CHUNK_TILES, (c + 1) * CHUNK_TILES)
             x_sb[c] = loads.tile([P, CHUNK_TILES * X_DIM], BF16, name="x_sb")
             nc.sync.dma_start(out=x_sb[c][:], in_=x_rows[:, c * CHUNK_TILES * X_DIM : (c + 1) * CHUNK_TILES * X_DIM])
             hf_sb[c] = loads.tile([P, CHUNK_TILES * HF_DIM], BF16, name="hf_sb")
             nc.sync.dma_start(
                 out=hf_sb[c][:], in_=hf_rows[:, c * CHUNK_TILES * HF_DIM : (c + 1) * CHUNK_TILES * HF_DIM]
             )
-            c_aggr_sb[c] = loads.tile([P, CHUNK_TILES, H_DIM], BF16, name="c_aggr_sb", bufs=4)
-            nc.sync.dma_start(out=c_aggr_sb[c][:], in_=c_aggr_rows[:, tiles, :])
-            diag[c] = loads.tile([P, CHUNK_TILES, P], F32, name="diag")
+
+        def load_c_aggr(c):
+            c_aggr_sb[c] = loads.tile([P, CHUNK_TILES, H_DIM], BF16, name="c_aggr_sb")
+            nc.sync.dma_start(out=c_aggr_sb[c][:], in_=c_aggr_rows[:, c * CHUNK_TILES : (c + 1) * CHUNK_TILES, :])
+
+        def mask_identity(c):
+            tiles = slice(c * CHUNK_TILES, (c + 1) * CHUNK_TILES)
             nc.gpsimd.tensor_tensor(
-                out=diag[c][:],
+                out=diag[:, tiles, :],
                 in0=ident[:].unsqueeze(1).to_broadcast([P, CHUNK_TILES, P]),
                 in1=mask_col[:, tiles].unsqueeze(2).to_broadcast([P, CHUNK_TILES, P]),
                 op=ALU.mult,
@@ -113,7 +118,7 @@ def tile_treelstmcell_pb_t_kernel(
                     for u in range(2):
                         if g == 0:
                             first = j * (X_DIM // 2) + u * WORDS
-                            words, perm = x_words[:, first : first + WORDS], diag[c][:, j, :]
+                            words, perm = x_words[:, first : first + WORDS], diag[:, c * CHUNK_TILES + j, :]
                         else:
                             first = j * (HF_DIM // 2) + (g - 1) * (K_PASS // 2) + u * WORDS
                             words, perm = hf_words[:, first : first + WORDS], ident[:]
@@ -195,7 +200,7 @@ def tile_treelstmcell_pb_t_kernel(
                 tiles = slice(half * BANK_TILES, (half + 1) * BANK_TILES)
                 back = transpose_back(i_times_u[c], 0, half)
                 nc.vector.tensor_tensor(out=c_new[c][:, tiles, :], in0=back[:], in1=c_aggr_sb[c][:, tiles, :], op=ALU.add)
-            nc.scalar.activation(out=tanh_c[c][:], in_=c_new[c][:], func=ACT.Tanh)
+                nc.scalar.activation(out=tanh_c[c][:, tiles, :], in_=c_new[c][:, tiles, :], func=ACT.Tanh)
             nc.sync.dma_start(out=c_rows[:, c * CHUNK_TILES : (c + 1) * CHUNK_TILES, :], in_=c_new[c][:])
 
         def hidden_state(c):
@@ -218,7 +223,7 @@ def tile_treelstmcell_pb_t_kernel(
             )
 
         def group_weights(g):
-            w_grouped[g] = wstage.tile([P, GATES, PACK], BF16, name="w_grouped", align_bytes=64)
+            w_grouped[g] = wstage.tile([P, GATES, PACK], BF16, name="w_grouped", align_bytes=64, bufs=2)
             nc.vector.tensor_copy(out=w_grouped[g][:], in_=w_raw[g][:].rearrange("q t c -> q c t"))
 
         def quantise_weights(g):
@@ -238,6 +243,12 @@ def tile_treelstmcell_pb_t_kernel(
         nc.sync.dma_start(out=bias_rows[GATE_TILES : 2 * GATE_TILES, :], in_=b_aggr_iou.rearrange("(m g) -> m g", g=P))
         nc.sync.dma_start(out=mask_all[:], in_=x_mask.partition_broadcast(P))
         load(1)
+        load(2)
+        load_c_aggr(0)
+        for c in range(CHUNKS):
+            mask_identity(c)
+        for c in range(CHUNKS):
+            order_mask(c)
 
         group_weights(0)
         for g in range(1, PASSES):
@@ -248,7 +259,7 @@ def tile_treelstmcell_pb_t_kernel(
         transpose_in(0, range(TP_BANKS))
         quantise(0, 0, 1)
         quantise(0, 1, 2)
-        order_mask(0)
+        transpose_in(1, range(0, TP_BANKS // 2))
 
         bias_ps = psum_bt.tile([P, P], BF16, name="bias_ps", tag="back")
         nc.tensor.transpose(bias_ps[:], bias_rows[:], ident_bf[:])
@@ -256,23 +267,24 @@ def tile_treelstmcell_pb_t_kernel(
         nc.vector.tensor_copy(out=bias_col[:], in_=bias_ps[:, 0 : 2 * GATE_TILES])
 
         for c in range(CHUNKS + 2):
-            if c + 2 < CHUNKS:
-                load(c + 2)
+            if c + 3 < CHUNKS:
+                load(c + 3)
             if c + 1 < CHUNKS:
-                order_mask(c + 1)
-                transpose_in(c + 1, range(0, TP_BANKS // 2))
+                load_c_aggr(c + 1)
             if 0 <= c - 2:
                 hidden_state(c - 2)
             if c + 1 < CHUNKS:
-                quantise(c + 1, 0, 1)
+                transpose_in(c + 1, range(TP_BANKS // 2, TP_BANKS))
             if c < CHUNKS:
                 gate_tiles(c, GATE_ORDER[0 : GATE_TILES // 2])
             if c + 1 < CHUNKS:
-                transpose_in(c + 1, range(TP_BANKS // 2, TP_BANKS))
+                quantise(c + 1, 0, 1)
+            if c + 2 < CHUNKS:
+                transpose_in(c + 2, range(0, TP_BANKS // 2))
             if 0 <= c - 1 < CHUNKS:
                 cell_state(c - 1)
+            if c + 1 < CHUNKS:
+                quantise(c + 1, 1, 2)
             if c < CHUNKS:
                 gate_tiles(c, GATE_ORDER[GATE_TILES // 2 :])
                 multiply_i_u(c)
-            if c + 1 < CHUNKS:
-                quantise(c + 1, 1, 2)

@@ -26,8 +26,8 @@ CHUNK_TILES = CHUNK // P
 CHUNKS = NODES // CHUNK
 WORDS = P
 BANK_TILES = 2
-TP_BANKS = PASSES * CHUNK_TILES // BANK_TILES
-GATE_ORDER = (0, 1, 4, 5, 2, 3)
+HALVES = CHUNK_TILES // BANK_TILES
+I_TILES, O_TILES, U_TILES = (0, 1), (2, 3), (4, 5)
 
 FLOPS = 2 * NODES * (X_DIM + HF_DIM) * GATES
 
@@ -67,7 +67,7 @@ def tile_treelstmcell_pb_t_kernel(
 
         mask_col = const.tile([P, NODE_TILES], BF16)
         nc.sync.dma_start(out=mask_col[:], in_=x_mask.rearrange("(p t) -> p t", t=NODE_TILES))
-        mask_all = const.tile([P, NODES], BF16)
+        mask_f32 = const.tile([P, NODE_TILES], F32)
         mask_row = const.tile([P, NODE_TILES, P], BF16)
 
         diag = const.tile([P, NODE_TILES, P], F32)
@@ -93,51 +93,44 @@ def tile_treelstmcell_pb_t_kernel(
                 op=ALU.mult,
             )
 
-        def order_mask(c):
-            tiles = slice(c * CHUNK_TILES, (c + 1) * CHUNK_TILES)
-            nc.gpsimd.tensor_scalar(
-                out=mask_row[:, tiles, :],
-                in0=mask_all[:].rearrange("q (p t) -> q t p", t=NODE_TILES)[:, tiles, :],
-                scalar1=1.0,
-                scalar2=0.0,
-                op0=ALU.mult,
-                op1=ALU.add,
-            )
+        def spread_mask(c):
+            spread = psum_z.tile([P, CHUNK_TILES, P], F32, name="spread", tag="sums")
+            for j in range(CHUNK_TILES):
+                t = c * CHUNK_TILES + j
+                nc.tensor.transpose(spread[:, j, :], mask_f32[:, t : t + 1].to_broadcast([P, P]), ident[:])
+            nc.scalar.copy(out=mask_row[:, c * CHUNK_TILES : (c + 1) * CHUNK_TILES, :], in_=spread[:])
 
-        def transpose_in(c, banks):
+        def transpose_in(c, g):
             if c not in a_grouped:
                 a_grouped[c] = acts.tile([P, PASSES * CHUNK * PACK], BF16, name="a_grouped", align_bytes=64)
-            x_words = x_sb[c][:].bitcast(F32)
-            hf_words = hf_sb[c][:].bitcast(F32)
+            if g == 0:
+                words, tile_words, first_word = x_sb[c][:].bitcast(F32), X_DIM // 2, 0
+            else:
+                words, tile_words, first_word = hf_sb[c][:].bitcast(F32), HF_DIM // 2, (g - 1) * (K_PASS // 2)
             grouped_words = a_grouped[c][:].bitcast(F32)
-            for b in banks:
-                g, half = divmod(b, CHUNK_TILES // BANK_TILES)
+            for half in range(HALVES):
                 kT = psum_tp.tile([P, 2, BANK_TILES * P], F32, name="kT")
                 for jj in range(BANK_TILES):
                     j = half * BANK_TILES + jj
                     for u in range(2):
-                        if g == 0:
-                            first = j * (X_DIM // 2) + u * WORDS
-                            words, perm = x_words[:, first : first + WORDS], diag[:, c * CHUNK_TILES + j, :]
-                        else:
-                            first = j * (HF_DIM // 2) + (g - 1) * (K_PASS // 2) + u * WORDS
-                            words, perm = hf_words[:, first : first + WORDS], ident[:]
-                        nc.tensor.transpose(kT[:, u, jj * P : (jj + 1) * P], words, perm)
+                        first = j * tile_words + first_word + u * WORDS
+                        perm = diag[:, c * CHUNK_TILES + j, :] if g == 0 else ident[:]
+                        nc.tensor.transpose(kT[:, u, jj * P : (jj + 1) * P], words[:, first : first + WORDS], perm)
                 first = (g * CHUNK + half * BANK_TILES * P) * 2
                 nc.scalar.copy(
                     out=grouped_words[:, first : first + BANK_TILES * P * 2].rearrange("p (n u) -> p n u", u=2),
                     in_=kT[:].rearrange("p u n -> p n u"),
                 )
 
-        def quantise(c, first_pass, passes):
+        def quantise(c, g):
             if c not in a_codes:
                 a_codes[c] = acts.tile([P, PASSES * CHUNK], U32, name="a_codes", align_bytes=64)
                 a_scales[c] = acts.tile([P, PASSES * CHUNK], U8, name="a_scales", align_bytes=64)
-            cols = slice(first_pass * CHUNK, (first_pass + passes) * CHUNK)
+            cols = slice(g * CHUNK, (g + 1) * CHUNK)
             nc.vector.quantize_mx(
                 out=a_codes[c][:, cols].bitcast(FP8X4),
                 scales=a_scales[c][:, cols],
-                in_=a_grouped[c][:, first_pass * CHUNK * PACK : (first_pass + passes) * CHUNK * PACK],
+                in_=a_grouped[c][:, g * CHUNK * PACK : (g + 1) * CHUNK * PACK],
             )
 
         def gate_tiles(c, some):
@@ -169,7 +162,7 @@ def tile_treelstmcell_pb_t_kernel(
                 nc.scalar.activation(
                     out=gates[c][:, m, :],
                     in_=masked[:],
-                    func=(ACT.Tanh if m >= 2 * H_TILES else ACT.Sigmoid),
+                    func=(ACT.Tanh if m in U_TILES else ACT.Sigmoid),
                     bias=bias_col[:, GATE_TILES + m : GATE_TILES + m + 1],
                     scale=1.0,
                 )
@@ -178,8 +171,8 @@ def tile_treelstmcell_pb_t_kernel(
             i_times_u[c] = work.tile([P, H_TILES, CHUNK], F32, name="i_times_u")
             nc.gpsimd.tensor_tensor(
                 out=i_times_u[c][:],
-                in0=gates[c][:, 0:H_TILES, :],
-                in1=gates[c][:, 2 * H_TILES : 3 * H_TILES, :],
+                in0=gates[c][:, I_TILES[0] : I_TILES[0] + H_TILES, :],
+                in1=gates[c][:, U_TILES[0] : U_TILES[0] + H_TILES, :],
                 op=ALU.mult,
             )
 
@@ -196,7 +189,7 @@ def tile_treelstmcell_pb_t_kernel(
         def cell_state(c):
             c_new[c] = work.tile([P, CHUNK_TILES, H_DIM], F32, name="c_new", bufs=3)
             tanh_c[c] = work.tile([P, CHUNK_TILES, H_DIM], F32, name="tanh_c")
-            for half in range(CHUNK_TILES // BANK_TILES):
+            for half in range(HALVES):
                 tiles = slice(half * BANK_TILES, (half + 1) * BANK_TILES)
                 back = transpose_back(i_times_u[c], 0, half)
                 nc.vector.tensor_tensor(out=c_new[c][:, tiles, :], in0=back[:], in1=c_aggr_sb[c][:, tiles, :], op=ALU.add)
@@ -205,9 +198,9 @@ def tile_treelstmcell_pb_t_kernel(
 
         def hidden_state(c):
             h_new = work.tile([P, CHUNK_TILES, H_DIM], F32, name="h_new", bufs=3)
-            for half in range(CHUNK_TILES // BANK_TILES):
+            for half in range(HALVES):
                 tiles = slice(half * BANK_TILES, (half + 1) * BANK_TILES)
-                back = transpose_back(gates[c], H_TILES, half)
+                back = transpose_back(gates[c], O_TILES[0], half)
                 nc.vector.tensor_tensor(out=h_new[:, tiles, :], in0=back[:], in1=tanh_c[c][:, tiles, :], op=ALU.mult)
             nc.sync.dma_start(out=h_rows[:, c * CHUNK_TILES : (c + 1) * CHUNK_TILES, :], in_=h_new[:])
 
@@ -236,19 +229,19 @@ def tile_treelstmcell_pb_t_kernel(
 
         bias_rows = const.tile([P, P], BF16)
         nc.vector.memset(bias_rows[:], 0.0)
+        nc.vector.tensor_copy(out=mask_f32[:], in_=mask_col[:])
         for g in range(PASSES):
             load_weights(g)
         load(0)
         nc.sync.dma_start(out=bias_rows[0:GATE_TILES, :], in_=b_iou_in.rearrange("(m g) -> m g", g=P))
         nc.sync.dma_start(out=bias_rows[GATE_TILES : 2 * GATE_TILES, :], in_=b_aggr_iou.rearrange("(m g) -> m g", g=P))
-        nc.sync.dma_start(out=mask_all[:], in_=x_mask.partition_broadcast(P))
         load(1)
         load(2)
         load_c_aggr(0)
+        mask_identity(0)
+        mask_identity(1)
         for c in range(CHUNKS):
-            mask_identity(c)
-        for c in range(CHUNKS):
-            order_mask(c)
+            spread_mask(c)
 
         group_weights(0)
         for g in range(1, PASSES):
@@ -256,35 +249,45 @@ def tile_treelstmcell_pb_t_kernel(
             quantise_weights(g - 1)
         quantise_weights(PASSES - 1)
 
-        transpose_in(0, range(TP_BANKS))
-        quantise(0, 0, 1)
-        quantise(0, 1, 2)
-        transpose_in(1, range(0, TP_BANKS // 2))
+        for g in range(PASSES):
+            transpose_in(0, g)
+        for g in range(PASSES):
+            quantise(0, g)
+        transpose_in(1, 0)
 
         bias_ps = psum_bt.tile([P, P], BF16, name="bias_ps", tag="back")
         nc.tensor.transpose(bias_ps[:], bias_rows[:], ident_bf[:])
         bias_col = const.tile([P, 2 * GATE_TILES], F32)
         nc.vector.tensor_copy(out=bias_col[:], in_=bias_ps[:, 0 : 2 * GATE_TILES])
 
-        for c in range(CHUNKS + 2):
+        for c in range(CHUNKS + 1):
             if c + 3 < CHUNKS:
                 load(c + 3)
             if c + 1 < CHUNKS:
                 load_c_aggr(c + 1)
-            if 0 <= c - 2:
-                hidden_state(c - 2)
-            if c + 1 < CHUNKS:
-                transpose_in(c + 1, range(TP_BANKS // 2, TP_BANKS))
-            if c < CHUNKS:
-                gate_tiles(c, GATE_ORDER[0 : GATE_TILES // 2])
-            if c + 1 < CHUNKS:
-                quantise(c + 1, 0, 1)
             if c + 2 < CHUNKS:
-                transpose_in(c + 2, range(0, TP_BANKS // 2))
-            if 0 <= c - 1 < CHUNKS:
+                mask_identity(c + 2)
+
+            if c + 1 < CHUNKS:
+                transpose_in(c + 1, 1)
+            if c < CHUNKS:
+                gate_tiles(c, I_TILES)
+
+            if 0 <= c - 1:
                 cell_state(c - 1)
             if c + 1 < CHUNKS:
-                quantise(c + 1, 1, 2)
+                transpose_in(c + 1, 2)
+                quantise(c + 1, 0)
+                quantise(c + 1, 1)
             if c < CHUNKS:
-                gate_tiles(c, GATE_ORDER[GATE_TILES // 2 :])
+                gate_tiles(c, U_TILES)
                 multiply_i_u(c)
+            if c + 1 < CHUNKS:
+                quantise(c + 1, 2)
+
+            if 0 <= c - 1:
+                hidden_state(c - 1)
+            if c + 2 < CHUNKS:
+                transpose_in(c + 2, 0)
+            if c < CHUNKS:
+                gate_tiles(c, O_TILES)

@@ -53,8 +53,6 @@ def tile_treelstmcell_pb_t_kernel(
         psum_z = ctx.enter_context(tc.psum_pool(name="psum_z", bufs=3))
         psum_bt = ctx.enter_context(tc.psum_pool(name="psum_bt", bufs=2))
 
-        ctx.enter_context(tc.manual_schedule())
-
         x_sb, hf_sb, c_aggr_sb = {}, {}, {}
         w_raw, w_grouped = {}, {}
         a_grouped, a_codes, a_scales = {}, {}, {}

@@ -53,6 +53,8 @@ def tile_treelstmcell_pb_t_kernel(
         psum_z = ctx.enter_context(tc.psum_pool(name="psum_z", bufs=3))
         psum_bt = ctx.enter_context(tc.psum_pool(name="psum_bt", bufs=2))
 
+        ctx.enter_context(tc.manual_schedule())
+
         x_sb, hf_sb, c_aggr_sb = {}, {}, {}
         w_raw, w_grouped = {}, {}
         a_grouped, a_codes, a_scales = {}, {}, {}
@@ -167,12 +169,14 @@ def tile_treelstmcell_pb_t_kernel(
 
         def multiply_i_u(c):
             i_times_u[c] = work.tile([P, H_TILES, CHUNK], F32, name="i_times_u")
-            nc.gpsimd.tensor_tensor(
-                out=i_times_u[c][:],
-                in0=gates[c][:, I_TILES[0] : I_TILES[0] + H_TILES, :],
-                in1=gates[c][:, U_TILES[0] : U_TILES[0] + H_TILES, :],
-                op=ALU.mult,
-            )
+            for half in range(HALVES):
+                cols = slice(half * BANK_TILES * P, (half + 1) * BANK_TILES * P)
+                nc.gpsimd.tensor_tensor(
+                    out=i_times_u[c][:, :, cols],
+                    in0=gates[c][:, I_TILES[0] : I_TILES[0] + H_TILES, cols],
+                    in1=gates[c][:, U_TILES[0] : U_TILES[0] + H_TILES, cols],
+                    op=ALU.mult,
+                )
 
         def transpose_back(source, first_tile, half):
             back = psum_bt.tile([P, BANK_TILES, H_DIM], F32, name="back")
@@ -192,7 +196,8 @@ def tile_treelstmcell_pb_t_kernel(
                 back = transpose_back(i_times_u[c], 0, half)
                 nc.vector.tensor_tensor(out=c_new[c][:, tiles, :], in0=back[:], in1=c_aggr_sb[c][:, tiles, :], op=ALU.add)
                 nc.scalar.activation(out=tanh_c[c][:, tiles, :], in_=c_new[c][:, tiles, :], func=ACT.Tanh)
-            nc.sync.dma_start(out=c_rows[:, c * CHUNK_TILES : (c + 1) * CHUNK_TILES, :], in_=c_new[c][:])
+                first = c * CHUNK_TILES + half * BANK_TILES
+                nc.sync.dma_start(out=c_rows[:, first : first + BANK_TILES, :], in_=c_new[c][:, tiles, :])
 
         def hidden_state(c):
             h_new = work.tile([P, CHUNK_TILES, H_DIM], F32, name="h_new", bufs=3)
@@ -200,7 +205,8 @@ def tile_treelstmcell_pb_t_kernel(
                 tiles = slice(half * BANK_TILES, (half + 1) * BANK_TILES)
                 back = transpose_back(gates[c], O_TILES[0], half)
                 nc.vector.tensor_tensor(out=h_new[:, tiles, :], in0=back[:], in1=tanh_c[c][:, tiles, :], op=ALU.mult)
-            nc.sync.dma_start(out=h_rows[:, c * CHUNK_TILES : (c + 1) * CHUNK_TILES, :], in_=h_new[:])
+                first = c * CHUNK_TILES + half * BANK_TILES
+                nc.sync.dma_start(out=h_rows[:, first : first + BANK_TILES, :], in_=h_new[:, tiles, :])
 
         w_codes = const.tile([P, PASSES * GATES], U32, align_bytes=64)
         w_scales = const.tile([P, PASSES * GATES], U8, align_bytes=64)

from contextlib import ExitStack

import concourse.mybir as mybir
from concourse.masks import make_identity

BF16 = mybir.dt.bfloat16
F32 = mybir.dt.float32
U32 = mybir.dt.uint32
U8 = mybir.dt.uint8
FP8X4 = mybir.dt.float8_e4m3fn_x4
ACT = mybir.ActivationFunctionType
ALU = mybir.AluOpType

P = 128
PACK = 4
K_PASS = P * PACK
NODES, X_DIM, CHILDREN, H_DIM = 4096, 512, 4, 256
HF_DIM = CHILDREN * H_DIM
GATES = 3 * H_DIM
PASSES = (X_DIM + HF_DIM) // K_PASS
GATE_TILES = GATES // P
H_TILES = H_DIM // P
NODE_TILES = NODES // P
CHUNK = 512
CHUNK_TILES = CHUNK // P
CHUNKS = NODES // CHUNK
WORDS = P
BANK_TILES = 2
HALVES = CHUNK_TILES // BANK_TILES
I_TILES, O_TILES, U_TILES = (0, 1), (2, 3), (4, 5)

FLOPS = 2 * NODES * (X_DIM + HF_DIM) * GATES


def tile_treelstmcell_pb_t_kernel(
    tc, x, x_mask, neighbour_h, c_aggr, W_iou_in, b_iou_in, W_aggr_iou, b_aggr_iou, out_0, out_1
):
    nc = tc.nc

    x_rows = x.rearrange("(p t) k -> p (t k)", t=NODE_TILES)
    hf_rows = neighbour_h.rearrange("(p t) c f -> p (t c f)", t=NODE_TILES)
    c_aggr_rows = c_aggr.rearrange("(p t) f -> p t f", t=NODE_TILES)
    h_rows = out_0.rearrange("(p t) f -> p t f", t=NODE_TILES)
    c_rows = out_1.rearrange("(p t) f -> p t f", t=NODE_TILES)

    with ExitStack() as ctx:
        const = ctx.enter_context(tc.tile_pool(name="const", bufs=1))
        wstage = ctx.enter_context(tc.tile_pool(name="wstage", bufs=3))
        loads = ctx.enter_context(tc.tile_pool(name="loads", bufs=3))
        acts = ctx.enter_context(tc.tile_pool(name="acts", bufs=2))
        work = ctx.enter_context(tc.tile_pool(name="work", bufs=2))
        psum_tp = ctx.enter_context(tc.psum_pool(name="psum_tp", bufs=3))
        psum_z = ctx.enter_context(tc.psum_pool(name="psum_z", bufs=3))
        psum_bt = ctx.enter_context(tc.psum_pool(name="psum_bt", bufs=2))

        ctx.enter_context(tc.manual_schedule())

        x_sb, hf_sb, c_aggr_sb = {}, {}, {}
        w_raw, w_grouped = {}, {}
        a_grouped, a_codes, a_scales = {}, {}, {}
        gates, i_times_u, c_new, tanh_c = {}, {}, {}, {}

        ident = const.tile([P, P], F32)
        make_identity(nc, ident[:])
        ident_bf = const.tile([P, P], BF16)
        make_identity(nc, ident_bf[:])

        mask_col = const.tile([P, NODE_TILES], BF16)
        nc.sync.dma_start(out=mask_col[:], in_=x_mask.rearrange("(p t) -> p t", t=NODE_TILES))
        mask_f32 = const.tile([P, NODE_TILES], F32)
        mask_row = const.tile([P, NODE_TILES, P], BF16)

        diag = const.tile([P, NODE_TILES, P], F32)

        def load(c):
            x_sb[c] = loads.tile([P, CHUNK_TILES * X_DIM], BF16, name="x_sb")
            nc.sync.dma_start(out=x_sb[c][:], in_=x_rows[:, c * CHUNK_TILES * X_DIM : (c + 1) * CHUNK_TILES * X_DIM])
            hf_sb[c] = loads.tile([P, CHUNK_TILES * HF_DIM], BF16, name="hf_sb")
            nc.sync.dma_start(
                out=hf_sb[c][:], in_=hf_rows[:, c * CHUNK_TILES * HF_DIM : (c + 1) * CHUNK_TILES * HF_DIM]
            )

        def load_c_aggr(c):
            c_aggr_sb[c] = loads.tile([P, CHUNK_TILES, H_DIM], BF16, name="c_aggr_sb")
            nc.sync.dma_start(out=c_aggr_sb[c][:], in_=c_aggr_rows[:, c * CHUNK_TILES : (c + 1) * CHUNK_TILES, :])

        def mask_identity(c):
            tiles = slice(c * CHUNK_TILES, (c + 1) * CHUNK_TILES)
            nc.gpsimd.tensor_tensor(
                out=diag[:, tiles, :],
                in0=ident[:].unsqueeze(1).to_broadcast([P, CHUNK_TILES, P]),
                in1=mask_col[:, tiles].unsqueeze(2).to_broadcast([P, CHUNK_TILES, P]),
                op=ALU.mult,
            )

        def spread_mask(c):
            spread = psum_z.tile([P, CHUNK_TILES, P], F32, name="spread", tag="sums")
            for j in range(CHUNK_TILES):
                t = c * CHUNK_TILES + j
                nc.tensor.transpose(spread[:, j, :], mask_f32[:, t : t + 1].to_broadcast([P, P]), ident[:])
            nc.scalar.copy(out=mask_row[:, c * CHUNK_TILES : (c + 1) * CHUNK_TILES, :], in_=spread[:])

        def transpose_in(c, g):
            if c not in a_grouped:
                a_grouped[c] = acts.tile([P, PASSES * CHUNK * PACK], BF16, name="a_grouped", align_bytes=64)
            if g == 0:
                words, tile_words, first_word = x_sb[c][:].bitcast(F32), X_DIM // 2, 0
            else:
                words, tile_words, first_word = hf_sb[c][:].bitcast(F32), HF_DIM // 2, (g - 1) * (K_PASS // 2)
            grouped_words = a_grouped[c][:].bitcast(F32)
            for half in range(HALVES):
                kT = psum_tp.tile([P, 2, BANK_TILES * P], F32, name="kT")
                for jj in range(BANK_TILES):
                    j = half * BANK_TILES + jj
                    for u in range(2):
                        first = j * tile_words + first_word + u * WORDS
                        perm = diag[:, c * CHUNK_TILES + j, :] if g == 0 else ident[:]
                        nc.tensor.transpose(kT[:, u, jj * P : (jj + 1) * P], words[:, first : first + WORDS], perm)
                first = (g * CHUNK + half * BANK_TILES * P) * 2
                nc.scalar.copy(
                    out=grouped_words[:, first : first + BANK_TILES * P * 2].rearrange("p (n u) -> p n u", u=2),
                    in_=kT[:].rearrange("p u n -> p n u"),
                )

        def quantise(c, g):
            if c not in a_codes:
                a_codes[c] = acts.tile([P, PASSES * CHUNK], U32, name="a_codes", align_bytes=64)
                a_scales[c] = acts.tile([P, PASSES * CHUNK], U8, name="a_scales", align_bytes=64)
            cols = slice(g * CHUNK, (g + 1) * CHUNK)
            nc.vector.quantize_mx(
                out=a_codes[c][:, cols].bitcast(FP8X4),
                scales=a_scales[c][:, cols],
                in_=a_grouped[c][:, g * CHUNK * PACK : (g + 1) * CHUNK * PACK],
            )

        def gate_tiles(c, some):
            if c not in gates:
                gates[c] = work.tile([P, GATE_TILES, CHUNK], F32, name="gates")
            for m in some:
                sums = psum_z.tile([P, CHUNK], F32, name="sums")
                for g in range(PASSES):
                    w_cols = slice(g * GATES + m * P, g * GATES + (m + 1) * P)
                    a_cols = slice(g * CHUNK, (g + 1) * CHUNK)
                    nc.tensor.matmul_mx(
                        out=sums[:],
                        lhsT=w_codes[:, w_cols].bitcast(FP8X4),
                        lhsT_scale=w_scales[:, w_cols],
                        rhs=a_codes[c][:, a_cols].bitcast(FP8X4),
                        rhs_scale=a_scales[c][:, a_cols],
                        start=(g == 0),
                        stop=(g == PASSES - 1),
                    )
                masked = work.tile([P, CHUNK], F32, name="masked", bufs=4)
                nc.vector.scalar_tensor_tensor(
                    out=masked[:],
                    in0=mask_row[:, c * CHUNK_TILES : (c + 1) * CHUNK_TILES, :].rearrange("q t p -> q (t p)"),
                    scalar=bias_col[:, m : m + 1],
                    in1=sums[:],
                    op0=ALU.mult,
                    op1=ALU.add,
                )
                nc.scalar.activation(
                    out=gates[c][:, m, :],
                    in_=masked[:],
                    func=(ACT.Tanh if m in U_TILES else ACT.Sigmoid),
                    bias=bias_col[:, GATE_TILES + m : GATE_TILES + m + 1],
                    scale=1.0,
                )

        def multiply_i_u(c):
            i_times_u[c] = work.tile([P, H_TILES, CHUNK], F32, name="i_times_u")
            for half in range(HALVES):
                cols = slice(half * BANK_TILES * P, (half + 1) * BANK_TILES * P)
                nc.gpsimd.tensor_tensor(
                    out=i_times_u[c][:, :, cols],
                    in0=gates[c][:, I_TILES[0] : I_TILES[0] + H_TILES, cols],
                    in1=gates[c][:, U_TILES[0] : U_TILES[0] + H_TILES, cols],
                    op=ALU.mult,
                )

        def transpose_back(source, first_tile, half):
            back = psum_bt.tile([P, BANK_TILES, H_DIM], F32, name="back")
            for jj in range(BANK_TILES):
                j = half * BANK_TILES + jj
                for f in range(H_TILES):
                    nc.tensor.transpose(
                        back[:, jj, f * P : (f + 1) * P], source[:, first_tile + f, j * P : (j + 1) * P], ident[:]
                    )
            return back

        def cell_state(c):
            c_new[c] = work.tile([P, CHUNK_TILES, H_DIM], F32, name="c_new", bufs=3)
            tanh_c[c] = work.tile([P, CHUNK_TILES, H_DIM], F32, name="tanh_c")
            for half in range(HALVES):
                tiles = slice(half * BANK_TILES, (half + 1) * BANK_TILES)
                back = transpose_back(i_times_u[c], 0, half)
                nc.vector.tensor_tensor(out=c_new[c][:, tiles, :], in0=back[:], in1=c_aggr_sb[c][:, tiles, :], op=ALU.add)
                nc.scalar.activation(out=tanh_c[c][:, tiles, :], in_=c_new[c][:, tiles, :], func=ACT.Tanh)
                first = c * CHUNK_TILES + half * BANK_TILES
                nc.sync.dma_start(out=c_rows[:, first : first + BANK_TILES, :], in_=c_new[c][:, tiles, :])

        def hidden_state(c):
            h_new = work.tile([P, CHUNK_TILES, H_DIM], F32, name="h_new", bufs=3)
            for half in range(HALVES):
                tiles = slice(half * BANK_TILES, (half + 1) * BANK_TILES)
                back = transpose_back(gates[c], O_TILES[0], half)
                nc.vector.tensor_tensor(out=h_new[:, tiles, :], in0=back[:], in1=tanh_c[c][:, tiles, :], op=ALU.mult)
                first = c * CHUNK_TILES + half * BANK_TILES
                nc.sync.dma_start(out=h_rows[:, first : first + BANK_TILES, :], in_=h_new[:, tiles, :])

        w_codes = const.tile([P, PASSES * GATES], U32, align_bytes=64)
        w_scales = const.tile([P, PASSES * GATES], U8, align_bytes=64)

        def load_weights(g):
            rows = W_iou_in if g == 0 else W_aggr_iou[(g - 1) * K_PASS : g * K_PASS, :]
            w_raw[g] = wstage.tile([P, PACK, GATES], BF16, name="w_raw")
            nc.sync.dma_start(
                out=w_raw[g][:].rearrange("q (u e) c -> q u (e c)", u=2),
                in_=rows.rearrange("(u q e) c -> q u (e c)", u=2, e=2),
            )

        def group_weights(g):
            w_grouped[g] = wstage.tile([P, GATES, PACK], BF16, name="w_grouped", align_bytes=64, bufs=2)
            nc.vector.tensor_copy(out=w_grouped[g][:], in_=w_raw[g][:].rearrange("q t c -> q c t"))

        def quantise_weights(g):
            for first, cols in ((0, 512), (512, 256)):
                nc.vector.quantize_mx(
                    out=w_codes[:, g * GATES + first : g * GATES + first + cols].bitcast(FP8X4),
                    scales=w_scales[:, g * GATES + first : g * GATES + first + cols],
                    in_=w_grouped[g][:].rearrange("q c t -> q (c t)")[:, first * PACK : (first + cols) * PACK],
                )

        bias_rows = const.tile([P, P], BF16)
        nc.vector.memset(bias_rows[:], 0.0)
        nc.vector.tensor_copy(out=mask_f32[:], in_=mask_col[:])
        for g in range(PASSES):
            load_weights(g)
        load(0)
        nc.sync.dma_start(out=bias_rows[0:GATE_TILES, :], in_=b_iou_in.rearrange("(m g) -> m g", g=P))
        nc.sync.dma_start(out=bias_rows[GATE_TILES : 2 * GATE_TILES, :], in_=b_aggr_iou.rearrange("(m g) -> m g", g=P))
        load(1)
        load(2)
        load_c_aggr(0)
        mask_identity(0)
        mask_identity(1)
        for c in range(CHUNKS):
            spread_mask(c)

        group_weights(0)
        for g in range(1, PASSES):
            group_weights(g)
            quantise_weights(g - 1)
        quantise_weights(PASSES - 1)

        for g in range(PASSES):
            transpose_in(0, g)
        for g in range(PASSES):
            quantise(0, g)
        transpose_in(1, 0)

        bias_ps = psum_bt.tile([P, P], BF16, name="bias_ps", tag="back")
        nc.tensor.transpose(bias_ps[:], bias_rows[:], ident_bf[:])
        bias_col = const.tile([P, 2 * GATE_TILES], F32)
        nc.vector.tensor_copy(out=bias_col[:], in_=bias_ps[:, 0 : 2 * GATE_TILES])

        for c in range(CHUNKS + 1):
            if c + 3 < CHUNKS:
                load(c + 3)
            if c + 1 < CHUNKS:
                load_c_aggr(c + 1)
            if c + 2 < CHUNKS:
                mask_identity(c + 2)

            if c + 1 < CHUNKS:
                transpose_in(c + 1, 1)
            if c < CHUNKS:
                gate_tiles(c, I_TILES)

            if 0 <= c - 1:
                cell_state(c - 1)
            if c + 1 < CHUNKS:
                transpose_in(c + 1, 2)
                quantise(c + 1, 0)
                quantise(c + 1, 1)
            if c < CHUNKS:
                gate_tiles(c, U_TILES)
                multiply_i_u(c)
            if c + 1 < CHUNKS:
                quantise(c + 1, 2)

            if 0 <= c - 1:
                hidden_state(c - 1)
            if c + 2 < CHUNKS:
                transpose_in(c + 2, 0)
            if c < CHUNKS:
                gate_tiles(c, O_TILES)
